import numpy as np
import ml_dtypes


def mxq(x, axis, fmt="e4m3"):
    dtype, down = {"e4m3": (ml_dtypes.float8_e4m3fn, 7), "e5m2": (ml_dtypes.float8_e5m2, 14)}[fmt]
    v = np.moveaxis(np.asarray(x, np.float32).astype(ml_dtypes.bfloat16).astype(np.float64), axis, -1)
    blocks = v.reshape(v.shape[:-1] + (-1, 32))
    amax = np.abs(blocks).max(-1, keepdims=True)
    byte = np.maximum(np.where(amax > 0, np.frexp(amax)[1] - 1 + 127, 0) - down, 1)
    scale = np.exp2(byte - 127.0)
    codes = (blocks / scale).astype(np.float32).astype(dtype).astype(np.float64)
    return np.moveaxis((codes * scale).reshape(v.shape), -1, axis)


WIDE = False


def mx_kscale(k):
    if not WIDE:
        return np.ones(k)
    levels = np.array([10, -10, 5, -5, 0])
    a = np.random.permutation(np.resize(levels, k // 512 * 4)).reshape(k // 512, 4)
    idx = np.arange(k)
    return np.exp2(a[idx // 512, idx % 128 // 32])


BF16 = ml_dtypes.bfloat16


def bf(x):
    return np.asarray(x, np.float32).astype(BF16)


def f64(x):
    return np.asarray(x).astype(np.float64)


E, C, H, I = 4, 2048, 512, 512


def erf(z):
    z = np.clip(z, -6.0, 6.0)
    y = 2.0 * z * z
    acc = np.ones_like(z)
    for n in range(100, 0, -1):
        acc = 1.0 + acc * y / (2 * n + 1)
    return np.clip(2.0 / np.sqrt(np.pi) * z * np.exp(-z * z) * acc, -1.0, 1.0)


def gelu_erf(v):
    return 0.5 * v * (1.0 + erf(v / np.sqrt(2.0)))


def setup_inputs():
    s = mx_kscale(H)
    return {"x": bf(np.random.standard_normal((E * C, H)) * s),
            "w1": bf(np.random.standard_normal((E, H, I)) / np.sqrt(H) / s[:, None]),
            "b1": bf(np.random.standard_normal((E, I)) * 0.3),
            "w2": bf(np.random.standard_normal((E, I, H)) * 1.5 / np.sqrt(I)),
            "b2": bf(np.random.standard_normal((E, H)) * 0.3)}


def reference(x, w1, b1, w2, b2):
    xe = f64(x).reshape(E, C, H)
    h = gelu_erf((mxq(xe, 2, "e4m3") @ mxq(f64(w1), 1, "e4m3")) + f64(b1)[:, None, :])
    out = (mxq(h, 2, "e4m3") @ mxq(f64(w2), 1, "e4m3")) + f64(b2)[:, None, :]
    return out.reshape(E * C, H)

@@ -1,0 +1,312 @@
+from contextlib import ExitStack
+
+import concourse.mybir as mybir
+from concourse.masks import make_identity
+
+F32 = mybir.dt.float32
+BF16 = mybir.dt.bfloat16
+U32 = mybir.dt.uint32
+U8 = mybir.dt.uint8
+FP8X4 = mybir.dt.float8_e4m3fn_x4
+ACT = mybir.ActivationFunctionType
+ALU = mybir.AluOpType
+
+E = 4
+C = 2048
+H = 512
+I = 512
+P = 128
+CH = 512
+NCH = E * C // CH
+PER_E = C // CH
+FLOPS = 2 * E * C * H * I * 2
+
+MANUAL = True
+S_GROUPS = 24
+
+
+def tile_fusedthorexpert_t_kernel(tc, x, w1, b1, w2, b2, out):
+    nc = tc.nc
+    with ExitStack() as ctx:
+        if MANUAL:
+            ctx.enter_context(tc.manual_schedule())
+        const = ctx.enter_context(tc.tile_pool(name="const", bufs=1))
+        xres = ctx.enter_context(tc.tile_pool(name="xres", bufs=1))
+        wres = ctx.enter_context(tc.tile_pool(name="wres", bufs=1))
+        wgp = ctx.enter_context(tc.tile_pool(name="wgp", bufs=2))
+        work = ctx.enter_context(tc.tile_pool(name="work", bufs=2))
+        obp = ctx.enter_context(tc.tile_pool(name="obp", bufs=4))
+        ps_x = ctx.enter_context(tc.psum_pool(name="ps_x", bufs=2))
+        ps_h = ctx.enter_context(tc.psum_pool(name="ps_h", bufs=3))
+        ps_o = ctx.enter_context(tc.psum_pool(name="ps_o", bufs=3))
+
+        identf = const.tile([P, P], F32, name="identf")
+        make_identity(nc, identf[:])
+        identb = const.tile([P, P], BF16, name="identb")
+        warm = const.tile([P, 1], F32, name="warm")
+        warm2 = const.tile([P, 1], F32, name="warm2")
+        b1raw = const.tile([P, P], BF16, name="b1raw")
+        b1t = const.tile([P, E * 4], F32, name="b1t")
+        b2b = const.tile([P, E * H], BF16, name="b2b")
+        nc.vector.memset(warm[:], 0.0)
+        nc.vector.memset(b1raw[:], 0.0)
+        nc.sync.dma_start(out=b1raw[0 : E * 4, :], in_=b1.rearrange("e (t p) -> (e t) p", p=P))
+        nc.scalar.activation(out=warm2[:], in_=warm[:], func=ACT.Gelu)
+        nc.vector.tensor_copy(out=identb[:], in_=identf[:])
+
+        xsb = {}
+        wraw = {}
+
+        def load_x(c):
+            t = xres.tile([P, 4 * H], BF16, name="x%d" % c)
+            nc.sync.dma_start(out=t[:], in_=x[c * CH : (c + 1) * CH, :].rearrange("(w r) k -> w (r k)", r=4))
+            xsb[c] = t
+
+        def load_w1(e):
+            t = wres.tile([P, 4 * I], BF16, name="w1raw%d" % e)
+            nc.sync.dma_start(
+                out=t[:].rearrange("p (u m) -> p u m", u=2),
+                in_=w1[e].rearrange("(u p f) i -> p u (f i)", u=2, f=2),
+            )
+            wraw[(1, e)] = t
+
+        def load_w2(e):
+            t = wres.tile([P, 4 * H], BF16, name="w2raw%d" % e)
+            nc.sync.dma_start(
+                out=t[:].rearrange("p (t h) -> p t h", t=4),
+                in_=w2[e].rearrange("(t p) h -> p t h", t=4),
+            )
+            wraw[(2, e)] = t
+
+        load_x(0)
+        load_w1(0)
+        load_x(1)
+        load_w2(0)
+        load_x(2)
+        load_w1(1)
+        nc.sync.dma_start(out=b2b[:], in_=b2.rearrange("e h -> (e h)").partition_broadcast(P))
+        load_x(3)
+        load_w2(1)
+        load_x(4)
+        load_x(5)
+        load_w1(2)
+        load_x(6)
+        load_w2(2)
+        load_x(7)
+        load_x(8)
+        load_w1(3)
+        load_x(9)
+        load_w2(3)
+        for c in range(10, NCH):
+            load_x(c)
+
+        def b1_spread():
+            b1ps = ps_h.tile([P, P], BF16, name="b1ps", tag="hp")
+            nc.tensor.transpose(b1ps[:], b1raw[:], identb[:])
+            nc.vector.tensor_copy(out=b1t[:], in_=b1ps[:, 0 : E * 4])
+
+        wg = {}
+        wcode = {}
+        wscale = {}
+
+        def regroup_views(dst, src):
+            d = dst[:].rearrange("p (c i j) -> p c j i", i=4, j=4)
+            s = src[:].rearrange("p (j c i) -> p c j i", j=4, i=4)
+            return d, s
+
+        def w_regroup(which, e, part, eng):
+            key = (which, e)
+            if key not in wg:
+                wg[key] = wgp.tile([P, 2048], BF16, name="wg", tag="wg", align_bytes=64)
+            d, s = regroup_views(wg[key], wraw[key])
+            if part is None:
+                lo, hi = 0, 128
+            else:
+                lo, hi = 64 * part, 64 * part + 64
+            if eng == "v":
+                nc.vector.tensor_copy(out=d[:, lo:hi], in_=s[:, lo:hi])
+            else:
+                nc.scalar.copy(out=d[:, lo:hi], in_=s[:, lo:hi])
+
+        def w_quant(which, e):
+            key = (which, e)
+            wcode[key] = wres.tile([P, 512], U32, name="wc%d_%d" % key, align_bytes=64)
+            wscale[key] = wres.tile([P, 512], U8, name="ws%d_%d" % key, align_bytes=64)
+            nc.vector.quantize_mx(out=wcode[key][:].bitcast(FP8X4), scales=wscale[key][:], in_=wg[key][:])
+
+        xt = {}
+        xg = {}
+        xc = {}
+        xs = {}
+        hp = {}
+        hb = {}
+        hg = {}
+        hc = {}
+        hs = {}
+        op = {}
+        ob = {}
+
+        def ok(c):
+            return 0 <= c < NCH
+
+        def tr(c):
+            if not ok(c):
+                return
+            xf = xsb[c][:].bitcast(F32)
+            for b in range(2):
+                t = ps_x.tile([P, 512], F32, name="xt", tag="xt")
+                for q in range(4):
+                    col = b * 512 + q * 128
+                    nc.tensor.transpose(t[:, q * 128 : (q + 1) * 128], xf[:, col : col + 128], identf[:])
+                xt[(c, b)] = t
+
+        def xexit(c):
+            if not ok(c):
+                return
+            xg[c] = work.tile([P, 2048], BF16, name="xg", tag="xg", align_bytes=64)
+            gf = xg[c][:].bitcast(F32)
+            for b in range(2):
+                nc.scalar.copy(
+                    out=gf[:, 512 * b : 512 * (b + 1)].rearrange("p (r w u) -> p r w u", r=2, u=2),
+                    in_=xt[(c, b)][:].rearrange("p (r u w) -> p r w u", r=2, u=2),
+                )
+
+        def qx(c):
+            if not ok(c):
+                return
+            xc[c] = work.tile([P, 512], U32, name="xc", tag="xc", align_bytes=64)
+            xs[c] = work.tile([P, 512], U8, name="xs", tag="xs", align_bytes=64)
+            nc.vector.quantize_mx(out=xc[c][:].bitcast(FP8X4), scales=xs[c][:], in_=xg[c][:])
+
+        def m1(c, t):
+            if not ok(c):
+                return
+            e = c // PER_E
+            hp[(c, t)] = ps_h.tile([P, 512], F32, name="hp", tag="hp")
+            nc.tensor.matmul_mx(
+                out=hp[(c, t)][:],
+                lhsT=wcode[(1, e)][:, t * P : (t + 1) * P].bitcast(FP8X4),
+                lhsT_scale=wscale[(1, e)][:, t * P : (t + 1) * P],
+                rhs=xc[c][:].bitcast(FP8X4),
+                rhs_scale=xs[c][:],
+                start=True,
+                stop=True,
+            )
+
+        def gelu(c, t):
+            if not ok(c):
+                return
+            e = c // PER_E
+            if t == 0:
+                hb[c] = work.tile([P, 2048], BF16, name="hb", tag="hb")
+            nc.scalar.activation(
+                out=hb[c][:, t * 512 : (t + 1) * 512],
+                in_=hp[(c, t)][:],
+                func=ACT.Gelu,
+                bias=b1t[:, 4 * e + t : 4 * e + t + 1],
+                scale=1.0,
+            )
+
+        def rg_s(c):
+            if not ok(c):
+                return
+            hg[c] = work.tile([P, 2048], BF16, name="hg", tag="hg", align_bytes=64)
+            if S_GROUPS > 0:
+                d, s = regroup_views(hg[c], hb[c])
+                nc.scalar.copy(out=d[:, 128 - S_GROUPS : 128], in_=s[:, 128 - S_GROUPS : 128])
+
+        def rg_v(c):
+            if not ok(c):
+                return
+            d, s = regroup_views(hg[c], hb[c])
+            nc.vector.tensor_copy(out=d[:, 0 : 128 - S_GROUPS], in_=s[:, 0 : 128 - S_GROUPS])
+
+        def qh(c):
+            if not ok(c):
+                return
+            hc[c] = work.tile([P, 512], U32, name="hc", tag="hc", align_bytes=64)
+            hs[c] = work.tile([P, 512], U8, name="hs", tag="hs", align_bytes=64)
+            nc.vector.quantize_mx(out=hc[c][:].bitcast(FP8X4), scales=hs[c][:], in_=hg[c][:])
+
+        def m2(c, r):
+            if not ok(c):
+                return
+            e = c // PER_E
+            op[(c, r)] = ps_o.tile([P, 512], F32, name="op", tag="op")
+            nc.tensor.matmul_mx(
+                out=op[(c, r)][:],
+                lhsT=hc[c][:, r * P : (r + 1) * P].bitcast(FP8X4),
+                lhsT_scale=hs[c][:, r * P : (r + 1) * P],
+                rhs=wcode[(2, e)][:].bitcast(FP8X4),
+                rhs_scale=wscale[(2, e)][:],
+                start=True,
+                stop=True,
+            )
+
+        def outx(c, r):
+            if not ok(c):
+                return
+            e = c // PER_E
+            if r == 0:
+                ob[c] = obp.tile([P, 4 * H], F32, name="ob", tag="ob")
+            nc.vector.tensor_tensor(
+                out=ob[c][:, r * H : (r + 1) * H],
+                in0=op[(c, r)][:],
+                in1=b2b[:, e * H : (e + 1) * H],
+                op=ALU.add,
+            )
+
+        def store(c, r0, r1):
+            if not ok(c):
+                return
+            dst = out[c * CH : (c + 1) * CH, :].rearrange("(w r) h -> w r h", r=4)
+            nc.sync.dma_start(
+                out=dst[:, r0:r1, :],
+                in_=ob[c][:, r0 * H : r1 * H].rearrange("p (r h) -> p r h", h=H),
+            )
+
+        for i in range(-4, NCH):
+            g, k = divmod(i + 5, 4)
+            prep = 1 <= g < E
+            rg_s(i + 1)
+            xexit(i + 3)
+            qx(i + 2)
+            if i == -4:
+                w_regroup(1, 0, None, "v")
+            if i == -2:
+                w_quant(1, 0)
+                w_regroup(2, 0, None, "v")
+            if i == -1:
+                w_quant(2, 0)
+            for r in range(3):
+                m2(i, r)
+            for t in range(3):
+                m1(i + 2, t)
+            outx(i, 0)
+            m2(i, 3)
+            outx(i, 1)
+            gelu(i + 2, 0)
+            m1(i + 2, 3)
+            for t in range(1, 4):
+                gelu(i + 2, t)
+            rg_v(i + 1)
+            if prep and k == 2:
+                w_quant(1, g)
+            if k == 0 and 2 <= g <= E:
+                w_quant(2, g - 1)
+            outx(i, 2)
+            if i == NCH - 1:
+                store(i, 0, 2)
+            qh(i + 1)
+            outx(i, 3)
+            if i == NCH - 1:
+                store(i, 2, 4)
+            else:
+                store(i, 0, 4)
+            tr(i + 4)
+            if i == -4:
+                b1_spread()
+            if prep and k < 2:
+                w_regroup(1, g, k, "s")
+            if prep and k >= 2:
+                w_regroup(2, g, k - 2, "s")

@@ -22,7 +22,7 @@ PER_E = C // CH
 FLOPS = 2 * E * C * H * I * 2
 
 MANUAL = True
-S_GROUPS = 24
+S_GROUPS = 36
 
 
 def tile_fusedthorexpert_t_kernel(tc, x, w1, b1, w2, b2, out):
@@ -35,6 +35,8 @@ def tile_fusedthorexpert_t_kernel(tc, x, w1, b1, w2, b2, out):
         wres = ctx.enter_context(tc.tile_pool(name="wres", bufs=1))
         wgp = ctx.enter_context(tc.tile_pool(name="wgp", bufs=2))
         work = ctx.enter_context(tc.tile_pool(name="work", bufs=2))
+        hbp = ctx.enter_context(tc.tile_pool(name="hbp", bufs=3))
+        one = ctx.enter_context(tc.tile_pool(name="one", bufs=1))
         obp = ctx.enter_context(tc.tile_pool(name="obp", bufs=4))
         ps_x = ctx.enter_context(tc.psum_pool(name="ps_x", bufs=2))
         ps_h = ctx.enter_context(tc.psum_pool(name="ps_h", bufs=3))
@@ -82,22 +84,19 @@ def tile_fusedthorexpert_t_kernel(tc, x, w1, b1, w2, b2, out):
         load_w1(0)
         load_x(1)
         load_w2(0)
-        load_x(2)
         load_w1(1)
-        nc.sync.dma_start(out=b2b[:], in_=b2.rearrange("e h -> (e h)").partition_broadcast(P))
-        load_x(3)
+        load_x(2)
         load_w2(1)
+        load_w1(2)
+        load_x(3)
+        load_w2(2)
+        nc.sync.dma_start(out=b2b[:], in_=b2.rearrange("e h -> (e h)").partition_broadcast(P))
         load_x(4)
         load_x(5)
-        load_w1(2)
-        load_x(6)
-        load_w2(2)
-        load_x(7)
-        load_x(8)
         load_w1(3)
-        load_x(9)
+        load_x(6)
         load_w2(3)
-        for c in range(10, NCH):
+        for c in range(7, NCH):
             load_x(c)
 
         def b1_spread():
@@ -140,7 +139,8 @@ def tile_fusedthorexpert_t_kernel(tc, x, w1, b1, w2, b2, out):
         xs = {}
         hp = {}
         hb = {}
-        hg = {}
+        hga = {}
+        hgb = {}
         hc = {}
         hs = {}
         op = {}
@@ -198,7 +198,7 @@ def tile_fusedthorexpert_t_kernel(tc, x, w1, b1, w2, b2, out):
                 return
             e = c // PER_E
             if t == 0:
-                hb[c] = work.tile([P, 2048], BF16, name="hb", tag="hb")
+                hb[c] = hbp.tile([P, 2048], BF16, name="hb", tag="hb")
             nc.scalar.activation(
                 out=hb[c][:, t * 512 : (t + 1) * 512],
                 in_=hp[(c, t)][:],
@@ -210,23 +210,39 @@ def tile_fusedthorexpert_t_kernel(tc, x, w1, b1, w2, b2, out):
         def rg_s(c):
             if not ok(c):
                 return
-            hg[c] = work.tile([P, 2048], BF16, name="hg", tag="hg", align_bytes=64)
+            hga[c] = work.tile([P, 1024], BF16, name="hga", tag="hga", align_bytes=64)
             if S_GROUPS > 0:
-                d, s = regroup_views(hg[c], hb[c])
-                nc.scalar.copy(out=d[:, 128 - S_GROUPS : 128], in_=s[:, 128 - S_GROUPS : 128])
+                d, s = regroup_views(hga[c], hb[c])
+                nc.scalar.copy(out=d[:, 64 - S_GROUPS : 64], in_=s[:, 64 - S_GROUPS : 64])
 
         def rg_v(c):
             if not ok(c):
                 return
-            d, s = regroup_views(hg[c], hb[c])
-            nc.vector.tensor_copy(out=d[:, 0 : 128 - S_GROUPS], in_=s[:, 0 : 128 - S_GROUPS])
+            d, s = regroup_views(hga[c], hb[c])
+            nc.vector.tensor_copy(out=d[:, 0 : 64 - S_GROUPS], in_=s[:, 0 : 64 - S_GROUPS])
 
-        def qh(c):
+        def rg_g(c):
             if not ok(c):
                 return
-            hc[c] = work.tile([P, 512], U32, name="hc", tag="hc", align_bytes=64)
-            hs[c] = work.tile([P, 512], U8, name="hs", tag="hs", align_bytes=64)
-            nc.vector.quantize_mx(out=hc[c][:].bitcast(FP8X4), scales=hs[c][:], in_=hg[c][:])
+            hgb[c] = one.tile([P, 1024], BF16, name="hgb", tag="hgb", align_bytes=64)
+            nc.gpsimd.tensor_scalar(
+                out=hgb[c][:].rearrange("p (n t) -> p n t", t=4),
+                in0=hb[c][:].rearrange("p (t n) -> p n t", t=4)[:, 256:512, :],
+                scalar1=1.0,
+                scalar2=0.0,
+                op0=ALU.mult,
+                op1=ALU.add,
+            )
+
+        def qh(c, half):
+            if not ok(c):
+                return
+            if half == 0:
+                hc[c] = work.tile([P, 512], U32, name="hc", tag="hc", align_bytes=64)
+                hs[c] = work.tile([P, 512], U8, name="hs", tag="hs", align_bytes=64)
+            src = hga[c] if half == 0 else hgb[c]
+            cols = slice(256 * half, 256 * half + 256)
+            nc.vector.quantize_mx(out=hc[c][:, cols].bitcast(FP8X4), scales=hs[c][:, cols], in_=src[:])
 
         def m2(c, r):
             if not ok(c):
@@ -265,48 +281,50 @@ def tile_fusedthorexpert_t_kernel(tc, x, w1, b1, w2, b2, out):
                 in_=ob[c][:, r0 * H : r1 * H].rearrange("p (r h) -> p r h", h=H),
             )
 
-        for i in range(-4, NCH):
-            g, k = divmod(i + 5, 4)
+        for i in range(-5, NCH):
+            g, k = divmod(i + 7, 4)
             prep = 1 <= g < E
-            rg_s(i + 1)
-            xexit(i + 3)
-            qx(i + 2)
-            if i == -4:
+            rg_s(i + 2)
+            xexit(i + 4)
+            rg_v(i + 1)
+            qx(i + 3)
+            if i == -5:
                 w_regroup(1, 0, None, "v")
-            if i == -2:
+            if i == -3:
                 w_quant(1, 0)
+            qh(i + 1, 0)
+            qh(i + 1, 1)
+            if i == -3:
                 w_regroup(2, 0, None, "v")
-            if i == -1:
+            if i == -2:
                 w_quant(2, 0)
-            for r in range(3):
-                m2(i, r)
+            if prep and k == 0:
+                w_regroup(1, g, None, "v")
+            if prep and k == 1:
+                w_quant(1, g)
+                w_regroup(2, g, None, "v")
+            if prep and k == 2:
+                w_quant(2, g)
+            rg_g(i + 2)
             for t in range(3):
-                m1(i + 2, t)
+                m1(i + 3, t)
             outx(i, 0)
             m2(i, 3)
-            outx(i, 1)
-            gelu(i + 2, 0)
-            m1(i + 2, 3)
+            gelu(i + 3, 0)
+            m1(i + 3, 3)
             for t in range(1, 4):
-                gelu(i + 2, t)
-            rg_v(i + 1)
-            if prep and k == 2:
-                w_quant(1, g)
-            if k == 0 and 2 <= g <= E:
-                w_quant(2, g - 1)
-            outx(i, 2)
+                gelu(i + 3, t)
+            outx(i, 1)
             if i == NCH - 1:
                 store(i, 0, 2)
-            qh(i + 1)
+            outx(i, 2)
             outx(i, 3)
             if i == NCH - 1:
                 store(i, 2, 4)
             else:
                 store(i, 0, 4)
-            tr(i + 4)
-            if i == -4:
+            tr(i + 5)
+            if i == -5:
                 b1_spread()
-            if prep and k < 2:
-                w_regroup(1, g, k, "s")
-            if prep and k >= 2:
-                w_regroup(2, g, k - 2, "s")
+            for r in range(3):
+                m2(i + 1, r)

@@ -21,7 +21,7 @@ NCH = E * C // CH
 PER_E = C // CH
 FLOPS = 2 * E * C * H * I * 2
 
-MANUAL = True
+MANUAL = False
 S_GROUPS = 36
 
 

@@ -21,8 +21,8 @@ NCH = E * C // CH
 PER_E = C // CH
 FLOPS = 2 * E * C * H * I * 2
 
-MANUAL = False
-S_GROUPS = 36
+MANUAL = True
+S_GROUPS = 44
 
 
 def tile_fusedthorexpert_t_kernel(tc, x, w1, b1, w2, b2, out):
@@ -49,7 +49,7 @@ def tile_fusedthorexpert_t_kernel(tc, x, w1, b1, w2, b2, out):
         warm2 = const.tile([P, 1], F32, name="warm2")
         b1raw = const.tile([P, P], BF16, name="b1raw")
         b1t = const.tile([P, E * 4], F32, name="b1t")
-        b2b = const.tile([P, E * H], BF16, name="b2b")
+        b2b = {}
         nc.vector.memset(warm[:], 0.0)
         nc.vector.memset(b1raw[:], 0.0)
         nc.sync.dma_start(out=b1raw[0 : E * 4, :], in_=b1.rearrange("e (t p) -> (e t) p", p=P))
@@ -80,24 +80,34 @@ def tile_fusedthorexpert_t_kernel(tc, x, w1, b1, w2, b2, out):
             )
             wraw[(2, e)] = t
 
+        def load_b2(e):
+            b2b[e] = const.tile([P, H], BF16, name="b2b%d" % e)
+            nc.sync.dma_start(out=b2b[e][:], in_=b2[e].partition_broadcast(P))
+
         load_x(0)
         load_w1(0)
         load_x(1)
         load_w2(0)
-        load_w1(1)
         load_x(2)
-        load_w2(1)
-        load_w1(2)
+        load_w1(1)
         load_x(3)
-        load_w2(2)
-        nc.sync.dma_start(out=b2b[:], in_=b2.rearrange("e h -> (e h)").partition_broadcast(P))
+        load_w2(1)
+        load_b2(0)
         load_x(4)
         load_x(5)
-        load_w1(3)
+        load_w1(2)
         load_x(6)
+        load_w2(2)
+        load_x(7)
+        load_x(8)
+        load_b2(1)
+        load_w1(3)
+        load_x(9)
         load_w2(3)
-        for c in range(7, NCH):
+        for c in range(10, NCH):
             load_x(c)
+        load_b2(2)
+        load_b2(3)
 
         def b1_spread():
             b1ps = ps_h.tile([P, P], BF16, name="b1ps", tag="hp")
@@ -268,7 +278,7 @@ def tile_fusedthorexpert_t_kernel(tc, x, w1, b1, w2, b2, out):
             nc.vector.tensor_tensor(
                 out=ob[c][:, r * H : (r + 1) * H],
                 in0=op[(c, r)][:],
-                in1=b2b[:, e * H : (e + 1) * H],
+                in1=b2b[e][:],
                 op=ALU.add,
             )
 
@@ -282,7 +292,7 @@ def tile_fusedthorexpert_t_kernel(tc, x, w1, b1, w2, b2, out):
             )
 
         for i in range(-5, NCH):
-            g, k = divmod(i + 7, 4)
+            g, k = divmod(i + 6, 4)
             prep = 1 <= g < E
             rg_s(i + 2)
             xexit(i + 4)
@@ -314,15 +324,21 @@ def tile_fusedthorexpert_t_kernel(tc, x, w1, b1, w2, b2, out):
             m1(i + 3, 3)
             for t in range(1, 4):
                 gelu(i + 3, t)
+            if i == NCH - 1:
+                store(i, 0, 1)
             outx(i, 1)
             if i == NCH - 1:
+                store(i, 1, 2)
+            else:
                 store(i, 0, 2)
             outx(i, 2)
+            if i == NCH - 1:
+                store(i, 2, 3)
             outx(i, 3)
             if i == NCH - 1:
-                store(i, 2, 4)
+                store(i, 3, 4)
             else:
-                store(i, 0, 4)
+                store(i, 2, 4)
             tr(i + 5)
             if i == -5:
                 b1_spread()

@@ -22,7 +22,16 @@ PER_E = C // CH
 FLOPS = 2 * E * C * H * I * 2
 
 MANUAL = True
-S_GROUPS = 44
+W_STEP = {-2: (1, 0), -1: (1, 1), 0: (1, 2), 1: (2, 1), 2: (2, 2), 6: (3, 0), 7: (3, 1), 8: (3, 2)}
+S_MID = 44
+
+
+def s_groups(c):
+    if c < 2:
+        return 0
+    if c >= NCH - 2:
+        return 64
+    return S_MID
 
 
 def tile_fusedthorexpert_t_kernel(tc, x, w1, b1, w2, b2, out):
@@ -93,18 +102,17 @@ def tile_fusedthorexpert_t_kernel(tc, x, w1, b1, w2, b2, out):
         load_x(3)
         load_w2(1)
         load_b2(0)
-        load_x(4)
-        load_x(5)
         load_w1(2)
-        load_x(6)
+        load_x(4)
         load_w2(2)
+        load_x(5)
+        load_x(6)
         load_x(7)
-        load_x(8)
-        load_b2(1)
         load_w1(3)
-        load_x(9)
+        load_x(8)
         load_w2(3)
-        for c in range(10, NCH):
+        load_b2(1)
+        for c in range(9, NCH):
             load_x(c)
         load_b2(2)
         load_b2(3)
@@ -221,15 +229,18 @@ def tile_fusedthorexpert_t_kernel(tc, x, w1, b1, w2, b2, out):
             if not ok(c):
                 return
             hga[c] = work.tile([P, 1024], BF16, name="hga", tag="hga", align_bytes=64)
-            if S_GROUPS > 0:
+            n = s_groups(c)
+            if n > 0:
                 d, s = regroup_views(hga[c], hb[c])
-                nc.scalar.copy(out=d[:, 64 - S_GROUPS : 64], in_=s[:, 64 - S_GROUPS : 64])
+                nc.scalar.copy(out=d[:, 64 - n : 64], in_=s[:, 64 - n : 64])
 
         def rg_v(c):
             if not ok(c):
                 return
-            d, s = regroup_views(hga[c], hb[c])
-            nc.vector.tensor_copy(out=d[:, 0 : 64 - S_GROUPS], in_=s[:, 0 : 64 - S_GROUPS])
+            n = s_groups(c)
+            if n < 64:
+                d, s = regroup_views(hga[c], hb[c])
+                nc.vector.tensor_copy(out=d[:, 0 : 64 - n], in_=s[:, 0 : 64 - n])
 
         def rg_g(c):
             if not ok(c):
@@ -292,8 +303,8 @@ def tile_fusedthorexpert_t_kernel(tc, x, w1, b1, w2, b2, out):
             )
 
         for i in range(-5, NCH):
-            g, k = divmod(i + 6, 4)
-            prep = 1 <= g < E
+            g, k = W_STEP.get(i, (0, 0))
+            prep = g > 0
             rg_s(i + 2)
             xexit(i + 4)
             rg_v(i + 1)
@@ -315,6 +326,8 @@ def tile_fusedthorexpert_t_kernel(tc, x, w1, b1, w2, b2, out):
                 w_regroup(2, g, None, "v")
             if prep and k == 2:
                 w_quant(2, g)
+            if i == 0:
+                w_regroup(1, 2, None, "v")
             rg_g(i + 2)
             for t in range(3):
                 m1(i + 3, t)

@@ -151,6 +151,15 @@ def tile_fusedthorexpert_t_kernel(tc, x, w1, b1, w2, b2, out):
             wscale[key] = wres.tile([P, 512], U8, name="ws%d_%d" % key, align_bytes=64)
             nc.vector.quantize_mx(out=wcode[key][:].bitcast(FP8X4), scales=wscale[key][:], in_=wg[key][:])
 
+        def w_prep(g, k):
+            if k == 0:
+                w_regroup(1, g, None, "v")
+            if k == 1:
+                w_quant(1, g)
+                w_regroup(2, g, None, "v")
+            if k == 2:
+                w_quant(2, g)
+
         xt = {}
         xg = {}
         xc = {}
@@ -304,9 +313,12 @@ def tile_fusedthorexpert_t_kernel(tc, x, w1, b1, w2, b2, out):
 
         for i in range(-5, NCH):
             g, k = W_STEP.get(i, (0, 0))
-            prep = g > 0
             rg_s(i + 2)
             xexit(i + 4)
+            if i >= -1 and g > 0:
+                w_prep(g, k)
+            if i == 0:
+                w_regroup(1, 2, None, "v")
             rg_v(i + 1)
             qx(i + 3)
             if i == -5:
@@ -319,15 +331,8 @@ def tile_fusedthorexpert_t_kernel(tc, x, w1, b1, w2, b2, out):
                 w_regroup(2, 0, None, "v")
             if i == -2:
                 w_quant(2, 0)
-            if prep and k == 0:
-                w_regroup(1, g, None, "v")
-            if prep and k == 1:
-                w_quant(1, g)
-                w_regroup(2, g, None, "v")
-            if prep and k == 2:
-                w_quant(2, g)
-            if i == 0:
-                w_regroup(1, 2, None, "v")
+            if i == -2:
+                w_prep(g, k)
             rg_g(i + 2)
             for t in range(3):
                 m1(i + 3, t)

@@ -23,15 +23,7 @@ FLOPS = 2 * E * C * H * I * 2
 
 MANUAL = True
 W_STEP = {-2: (1, 0), -1: (1, 1), 0: (1, 2), 1: (2, 1), 2: (2, 2), 6: (3, 0), 7: (3, 1), 8: (3, 2)}
-S_MID = 44
-
-
-def s_groups(c):
-    if c < 2:
-        return 0
-    if c >= NCH - 2:
-        return 64
-    return S_MID
+WS = 128
 
 
 def tile_fusedthorexpert_t_kernel(tc, x, w1, b1, w2, b2, out):
@@ -237,27 +229,17 @@ def tile_fusedthorexpert_t_kernel(tc, x, w1, b1, w2, b2, out):
         def rg_s(c):
             if not ok(c):
                 return
-            hga[c] = work.tile([P, 1024], BF16, name="hga", tag="hga", align_bytes=64)
-            n = s_groups(c)
-            if n > 0:
-                d, s = regroup_views(hga[c], hb[c])
-                nc.scalar.copy(out=d[:, 64 - n : 64], in_=s[:, 64 - n : 64])
-
-        def rg_v(c):
-            if not ok(c):
-                return
-            n = s_groups(c)
-            if n < 64:
-                d, s = regroup_views(hga[c], hb[c])
-                nc.vector.tensor_copy(out=d[:, 0 : 64 - n], in_=s[:, 0 : 64 - n])
+            hga[c] = work.tile([P, 4 * WS], BF16, name="hga", tag="hga", align_bytes=64)
+            d, s = regroup_views(hga[c], hb[c])
+            nc.scalar.copy(out=d, in_=s[:, 0 : WS // 4])
 
         def rg_g(c):
             if not ok(c):
                 return
-            hgb[c] = one.tile([P, 1024], BF16, name="hgb", tag="hgb", align_bytes=64)
+            hgb[c] = one.tile([P, 2048 - 4 * WS], BF16, name="hgb", tag="hgb", align_bytes=64)
             nc.gpsimd.tensor_scalar(
                 out=hgb[c][:].rearrange("p (n t) -> p n t", t=4),
-                in0=hb[c][:].rearrange("p (t n) -> p n t", t=4)[:, 256:512, :],
+                in0=hb[c][:].rearrange("p (t n) -> p n t", t=4)[:, WS:512, :],
                 scalar1=1.0,
                 scalar2=0.0,
                 op0=ALU.mult,
@@ -270,9 +252,15 @@ def tile_fusedthorexpert_t_kernel(tc, x, w1, b1, w2, b2, out):
             if half == 0:
                 hc[c] = work.tile([P, 512], U32, name="hc", tag="hc", align_bytes=64)
                 hs[c] = work.tile([P, 512], U8, name="hs", tag="hs", align_bytes=64)
-            src = hga[c] if half == 0 else hgb[c]
-            cols = slice(256 * half, 256 * half + 256)
-            nc.vector.quantize_mx(out=hc[c][:, cols].bitcast(FP8X4), scales=hs[c][:, cols], in_=src[:])
+                pieces = [(0, WS, hga[c], 0)]
+            else:
+                pieces = [(128, 256, hgb[c], 0), (384, 128, hgb[c], 1024)]
+            for w0, w, src, at in pieces:
+                nc.vector.quantize_mx(
+                    out=hc[c][:, w0 : w0 + w].bitcast(FP8X4),
+                    scales=hs[c][:, w0 : w0 + w],
+                    in_=src[:, at : at + 4 * w],
+                )
 
         def m2(c, r):
             if not ok(c):
@@ -319,7 +307,6 @@ def tile_fusedthorexpert_t_kernel(tc, x, w1, b1, w2, b2, out):
                 w_prep(g, k)
             if i == 0:
                 w_regroup(1, 2, None, "v")
-            rg_v(i + 1)
             qx(i + 3)
             if i == -5:
                 w_regroup(1, 0, None, "v")

@@ -50,10 +50,15 @@ def tile_fusedthorexpert_t_kernel(tc, x, w1, b1, w2, b2, out):
         warm2 = const.tile([P, 1], F32, name="warm2")
         b1raw = const.tile([P, P], BF16, name="b1raw")
         b1t = const.tile([P, E * 4], F32, name="b1t")
+        b2raw = const.tile([P, E * H], BF16, name="b2raw")
+        ones = const.tile([P, P], BF16, name="ones")
         b2b = {}
         nc.vector.memset(warm[:], 0.0)
         nc.vector.memset(b1raw[:], 0.0)
+        nc.vector.memset(b2raw[:], 0.0)
+        nc.vector.memset(ones[:], 1.0)
         nc.sync.dma_start(out=b1raw[0 : E * 4, :], in_=b1.rearrange("e (t p) -> (e t) p", p=P))
+        nc.sync.dma_start(out=b2raw[0:1, :], in_=b2.rearrange("(o e) h -> o (e h)", o=1))
         nc.scalar.activation(out=warm2[:], in_=warm[:], func=ACT.Gelu)
         nc.vector.tensor_copy(out=identb[:], in_=identf[:])
 
@@ -81,10 +86,6 @@ def tile_fusedthorexpert_t_kernel(tc, x, w1, b1, w2, b2, out):
             )
             wraw[(2, e)] = t
 
-        def load_b2(e):
-            b2b[e] = const.tile([P, H], BF16, name="b2b%d" % e)
-            nc.sync.dma_start(out=b2b[e][:], in_=b2[e].partition_broadcast(P))
-
         load_x(0)
         load_w1(0)
         load_x(1)
@@ -93,21 +94,18 @@ def tile_fusedthorexpert_t_kernel(tc, x, w1, b1, w2, b2, out):
         load_w1(1)
         load_x(3)
         load_w2(1)
-        load_b2(0)
-        load_w1(2)
         load_x(4)
-        load_w2(2)
+        load_w1(2)
         load_x(5)
+        load_w2(2)
         load_x(6)
         load_x(7)
-        load_w1(3)
-        load_x(8)
-        load_w2(3)
-        load_b2(1)
-        for c in range(9, NCH):
-            load_x(c)
-        load_b2(2)
-        load_b2(3)
+
+        def b2_spread(e):
+            b2ps = ps_h.tile([P, H], F32, name="b2ps", tag="hp")
+            nc.tensor.matmul(b2ps[:], lhsT=ones[:], rhs=b2raw[:, e * H : (e + 1) * H], start=True, stop=True)
+            b2b[e] = const.tile([P, H], BF16, name="b2b%d" % e)
+            nc.scalar.copy(out=b2b[e][:], in_=b2ps[:])
 
         def b1_spread():
             b1ps = ps_h.tile([P, P], BF16, name="b1ps", tag="hp")
@@ -344,8 +342,17 @@ def tile_fusedthorexpert_t_kernel(tc, x, w1, b1, w2, b2, out):
                 store(i, 3, 4)
             else:
                 store(i, 2, 4)
+            if i == -5:
+                for e in range(E):
+                    b2_spread(e)
             tr(i + 5)
             if i == -5:
                 b1_spread()
+            if i >= 0 and i + 8 < NCH:
+                load_x(i + 8)
+            if i == 1:
+                load_w1(3)
+            if i == 2:
+                load_w2(3)
             for r in range(3):
                 m2(i + 1, r)

@@ -50,15 +50,13 @@ def tile_fusedthorexpert_t_kernel(tc, x, w1, b1, w2, b2, out):
         warm2 = const.tile([P, 1], F32, name="warm2")
         b1raw = const.tile([P, P], BF16, name="b1raw")
         b1t = const.tile([P, E * 4], F32, name="b1t")
-        b2raw = const.tile([P, E * H], BF16, name="b2raw")
-        ones = const.tile([P, P], BF16, name="ones")
+        b2raw = const.tile([P, H], BF16, name="b2raw")
         b2b = {}
         nc.vector.memset(warm[:], 0.0)
         nc.vector.memset(b1raw[:], 0.0)
-        nc.vector.memset(b2raw[:], 0.0)
-        nc.vector.memset(ones[:], 1.0)
+        nc.vector.memset(b2raw[:].bitcast(U32), 0)
         nc.sync.dma_start(out=b1raw[0 : E * 4, :], in_=b1.rearrange("e (t p) -> (e t) p", p=P))
-        nc.sync.dma_start(out=b2raw[0:1, :], in_=b2.rearrange("(o e) h -> o (e h)", o=1))
+        nc.sync.dma_start(out=b2raw[0:E, :], in_=b2[:, :])
         nc.scalar.activation(out=warm2[:], in_=warm[:], func=ACT.Gelu)
         nc.vector.tensor_copy(out=identb[:], in_=identf[:])
 
@@ -103,7 +101,9 @@ def tile_fusedthorexpert_t_kernel(tc, x, w1, b1, w2, b2, out):
 
         def b2_spread(e):
             b2ps = ps_h.tile([P, H], F32, name="b2ps", tag="hp")
-            nc.tensor.matmul(b2ps[:], lhsT=ones[:], rhs=b2raw[:, e * H : (e + 1) * H], start=True, stop=True)
+            nc.tensor.matmul(
+                b2ps[:], lhsT=identb[:, e : e + 1].to_broadcast([P, P]), rhs=b2raw[:], start=True, stop=True
+            )
             b2b[e] = const.tile([P, H], BF16, name="b2b%d" % e)
             nc.scalar.copy(out=b2b[e][:], in_=b2ps[:])
 

@@ -22,8 +22,14 @@ PER_E = C // CH
 FLOPS = 2 * E * C * H * I * 2
 
 MANUAL = True
-W_STEP = {-2: (1, 0), -1: (1, 1), 0: (1, 2), 1: (2, 1), 2: (2, 2), 6: (3, 0), 7: (3, 1), 8: (3, 2)}
-WS = 128
+HEAD = 2
+W_V = 96
+W_V1 = 128
+
+
+def s_tokens(c):
+    return 256 if c >= NCH - TAILN else 128
+TAILN = 1
 
 
 def tile_fusedthorexpert_t_kernel(tc, x, w1, b1, w2, b2, out):
@@ -50,13 +56,10 @@ def tile_fusedthorexpert_t_kernel(tc, x, w1, b1, w2, b2, out):
         warm2 = const.tile([P, 1], F32, name="warm2")
         b1raw = const.tile([P, P], BF16, name="b1raw")
         b1t = const.tile([P, E * 4], F32, name="b1t")
-        b2raw = const.tile([P, H], BF16, name="b2raw")
         b2b = {}
         nc.vector.memset(warm[:], 0.0)
         nc.vector.memset(b1raw[:], 0.0)
-        nc.vector.memset(b2raw[:].bitcast(U32), 0)
         nc.sync.dma_start(out=b1raw[0 : E * 4, :], in_=b1.rearrange("e (t p) -> (e t) p", p=P))
-        nc.sync.dma_start(out=b2raw[0:E, :], in_=b2[:, :])
         nc.scalar.activation(out=warm2[:], in_=warm[:], func=ACT.Gelu)
         nc.vector.tensor_copy(out=identb[:], in_=identf[:])
 
@@ -67,6 +70,15 @@ def tile_fusedthorexpert_t_kernel(tc, x, w1, b1, w2, b2, out):
             t = xres.tile([P, 4 * H], BF16, name="x%d" % c)
             nc.sync.dma_start(out=t[:], in_=x[c * CH : (c + 1) * CH, :].rearrange("(w r) k -> w (r k)", r=4))
             xsb[c] = t
+
+        def load_x_half(c, b):
+            if b == 0:
+                xsb[c] = xres.tile([P, 4 * H], BF16, name="x%d" % c)
+            src = x[c * CH : (c + 1) * CH, :].rearrange("(w r) k -> w r k", r=4)
+            nc.sync.dma_start(
+                out=xsb[c][:, 2 * b * H : 2 * (b + 1) * H].rearrange("p (r k) -> p r k", r=2),
+                in_=src[:, 2 * b : 2 * (b + 1), :],
+            )
 
         def load_w1(e):
             t = wres.tile([P, 4 * I], BF16, name="w1raw%d" % e)
@@ -84,28 +96,26 @@ def tile_fusedthorexpert_t_kernel(tc, x, w1, b1, w2, b2, out):
             )
             wraw[(2, e)] = t
 
-        load_x(0)
+        def load_b2(e):
+            b2b[e] = const.tile([P, H], BF16, name="b2b%d" % e)
+            nc.sync.dma_start(out=b2b[e][:], in_=b2[e].partition_broadcast(P))
+
+        load_x_half(0, 0)
         load_w1(0)
+        load_x_half(0, 1)
         load_x(1)
         load_w2(0)
         load_x(2)
         load_w1(1)
         load_x(3)
         load_w2(1)
+        load_b2(0)
         load_x(4)
         load_w1(2)
         load_x(5)
         load_w2(2)
         load_x(6)
         load_x(7)
-
-        def b2_spread(e):
-            b2ps = ps_h.tile([P, H], F32, name="b2ps", tag="hp")
-            nc.tensor.matmul(
-                b2ps[:], lhsT=identb[:, e : e + 1].to_broadcast([P, P]), rhs=b2raw[:], start=True, stop=True
-            )
-            b2b[e] = const.tile([P, H], BF16, name="b2b%d" % e)
-            nc.scalar.copy(out=b2b[e][:], in_=b2ps[:])
 
         def b1_spread():
             b1ps = ps_h.tile([P, P], BF16, name="b1ps", tag="hp")
@@ -121,15 +131,13 @@ def tile_fusedthorexpert_t_kernel(tc, x, w1, b1, w2, b2, out):
             s = src[:].rearrange("p (j c i) -> p c j i", j=4, i=4)
             return d, s
 
-        def w_regroup(which, e, part, eng):
+        def w_regroup(which, e, eng, lo, hi):
             key = (which, e)
             if key not in wg:
                 wg[key] = wgp.tile([P, 2048], BF16, name="wg", tag="wg", align_bytes=64)
+            if lo >= hi:
+                return
             d, s = regroup_views(wg[key], wraw[key])
-            if part is None:
-                lo, hi = 0, 128
-            else:
-                lo, hi = 64 * part, 64 * part + 64
             if eng == "v":
                 nc.vector.tensor_copy(out=d[:, lo:hi], in_=s[:, lo:hi])
             else:
@@ -141,14 +149,19 @@ def tile_fusedthorexpert_t_kernel(tc, x, w1, b1, w2, b2, out):
             wscale[key] = wres.tile([P, 512], U8, name="ws%d_%d" % key, align_bytes=64)
             nc.vector.quantize_mx(out=wcode[key][:].bitcast(FP8X4), scales=wscale[key][:], in_=wg[key][:])
 
-        def w_prep(g, k):
-            if k == 0:
-                w_regroup(1, g, None, "v")
-            if k == 1:
-                w_quant(1, g)
-                w_regroup(2, g, None, "v")
-            if k == 2:
-                w_quant(2, g)
+        def w_prep(i, eng):
+            g, k = (i + 6) // 4, (i + 6) % 4
+            if not 1 <= g < E:
+                return
+            which = 1 + k // 2
+            wv = W_V if g > 1 else W_V1
+            if k % 2 == 0:
+                if eng == "v":
+                    w_regroup(which, g, "v", 0, wv)
+                else:
+                    w_regroup(which, g, "s", wv, 128)
+            elif eng == "v":
+                w_quant(which, g)
 
         xt = {}
         xg = {}
@@ -227,22 +240,33 @@ def tile_fusedthorexpert_t_kernel(tc, x, w1, b1, w2, b2, out):
         def rg_s(c):
             if not ok(c):
                 return
-            hga[c] = work.tile([P, 4 * WS], BF16, name="hga", tag="hga", align_bytes=64)
+            hga[c] = work.tile([P, 1024], BF16, name="hga", tag="hga", align_bytes=64)
             d, s = regroup_views(hga[c], hb[c])
-            nc.scalar.copy(out=d, in_=s[:, 0 : WS // 4])
+            n = s_tokens(c) // 4
+            nc.scalar.copy(out=d[:, 0:n], in_=s[:, 0:n])
+
+        def rg_v(c):
+            if not ok(c) or c >= HEAD:
+                return
+            hgb[c] = one.tile([P, 1024], BF16, name="hgb", tag="hgb", align_bytes=64)
+            d, s = regroup_views(hga[c], hb[c])
+            n = s_tokens(c) // 4
+            nc.vector.tensor_copy(out=d[:, n:64], in_=s[:, n:64])
+            d, s = regroup_views(hgb[c], hb[c])
+            nc.vector.tensor_copy(out=d, in_=s[:, 64:128])
+
+        def g_copy(dst, src):
+            nc.gpsimd.tensor_scalar(out=dst, in0=src, scalar1=1.0, scalar2=0.0, op0=ALU.mult, op1=ALU.add)
 
         def rg_g(c):
-            if not ok(c):
+            if not ok(c) or c < HEAD:
                 return
-            hgb[c] = one.tile([P, 2048 - 4 * WS], BF16, name="hgb", tag="hgb", align_bytes=64)
-            nc.gpsimd.tensor_scalar(
-                out=hgb[c][:].rearrange("p (n t) -> p n t", t=4),
-                in0=hb[c][:].rearrange("p (t n) -> p n t", t=4)[:, WS:512, :],
-                scalar1=1.0,
-                scalar2=0.0,
-                op0=ALU.mult,
-                op1=ALU.add,
-            )
+            hgb[c] = one.tile([P, 1024], BF16, name="hgb", tag="hgb", align_bytes=64)
+            s = hb[c][:].rearrange("p (t n) -> p n t", t=4)
+            g_copy(hgb[c][:].rearrange("p (n t) -> p n t", t=4), s[:, 256:512, :])
+            n = s_tokens(c)
+            if n < 256:
+                g_copy(hga[c][:].rearrange("p (n t) -> p n t", t=4)[:, n:256, :], s[:, n:256, :])
 
         def qh(c, half):
             if not ok(c):
@@ -250,15 +274,9 @@ def tile_fusedthorexpert_t_kernel(tc, x, w1, b1, w2, b2, out):
             if half == 0:
                 hc[c] = work.tile([P, 512], U32, name="hc", tag="hc", align_bytes=64)
                 hs[c] = work.tile([P, 512], U8, name="hs", tag="hs", align_bytes=64)
-                pieces = [(0, WS, hga[c], 0)]
-            else:
-                pieces = [(128, 256, hgb[c], 0), (384, 128, hgb[c], 1024)]
-            for w0, w, src, at in pieces:
-                nc.vector.quantize_mx(
-                    out=hc[c][:, w0 : w0 + w].bitcast(FP8X4),
-                    scales=hs[c][:, w0 : w0 + w],
-                    in_=src[:, at : at + 4 * w],
-                )
+            src = hga[c] if half == 0 else hgb[c]
+            cols = slice(256 * half, 256 * half + 256)
+            nc.vector.quantize_mx(out=hc[c][:, cols].bitcast(FP8X4), scales=hs[c][:, cols], in_=src[:])
 
         def m2(c, r):
             if not ok(c):
@@ -297,28 +315,31 @@ def tile_fusedthorexpert_t_kernel(tc, x, w1, b1, w2, b2, out):
                 in_=ob[c][:, r0 * H : r1 * H].rearrange("p (r h) -> p r h", h=H),
             )
 
+        b1_spread()
         for i in range(-5, NCH):
-            g, k = W_STEP.get(i, (0, 0))
-            rg_s(i + 2)
             xexit(i + 4)
-            if i >= -1 and g > 0:
-                w_prep(g, k)
-            if i == 0:
-                w_regroup(1, 2, None, "v")
-            qx(i + 3)
-            if i == -5:
-                w_regroup(1, 0, None, "v")
+            rg_s(i + 2)
+            w_prep(i, "s")
+            if i >= -1:
+                w_prep(i, "v")
+            rg_v(i + 1)
             if i == -3:
                 w_quant(1, 0)
+            qx(i + 3)
+            if i == -5:
+                w_regroup(1, 0, "v", 0, 128)
             qh(i + 1, 0)
             qh(i + 1, 1)
             if i == -3:
-                w_regroup(2, 0, None, "v")
+                w_regroup(2, 0, "v", 0, 128)
             if i == -2:
                 w_quant(2, 0)
             if i == -2:
-                w_prep(g, k)
+                w_prep(i, "v")
             rg_g(i + 2)
+            if i == -1:
+                for r in range(3):
+                    m2(0, r)
             for t in range(3):
                 m1(i + 3, t)
             outx(i, 0)
@@ -342,17 +363,15 @@ def tile_fusedthorexpert_t_kernel(tc, x, w1, b1, w2, b2, out):
                 store(i, 3, 4)
             else:
                 store(i, 2, 4)
-            if i == -5:
-                for e in range(E):
-                    b2_spread(e)
             tr(i + 5)
-            if i == -5:
-                b1_spread()
             if i >= 0 and i + 8 < NCH:
                 load_x(i + 8)
+            if i >= 0 and i % 4 == 0 and i // 4 + 1 < E:
+                load_b2(i // 4 + 1)
             if i == 1:
                 load_w1(3)
             if i == 2:
                 load_w2(3)
-            for r in range(3):
-                m2(i + 1, r)
+            if i >= 0:
+                for r in range(3):
+                    m2(i + 1, r)

@@ -23,13 +23,11 @@ FLOPS = 2 * E * C * H * I * 2
 
 MANUAL = True
 HEAD = 2
-W_V = 96
+W_V = 80
 W_V1 = 128
-
-
-def s_tokens(c):
-    return 256 if c >= NCH - TAILN else 128
-TAILN = 1
+N_S = 96
+N_V = 32
+N_A = N_S + N_V
 
 
 def tile_fusedthorexpert_t_kernel(tc, x, w1, b1, w2, b2, out):
@@ -240,43 +238,57 @@ def tile_fusedthorexpert_t_kernel(tc, x, w1, b1, w2, b2, out):
         def rg_s(c):
             if not ok(c):
                 return
-            hga[c] = work.tile([P, 1024], BF16, name="hga", tag="hga", align_bytes=64)
+            hga[c] = work.tile([P, 4 * N_A], BF16, name="hga", tag="hga", align_bytes=64)
             d, s = regroup_views(hga[c], hb[c])
-            n = s_tokens(c) // 4
-            nc.scalar.copy(out=d[:, 0:n], in_=s[:, 0:n])
+            nc.scalar.copy(out=d[:, 0 : N_S // 4], in_=s[:, 0 : N_S // 4])
 
         def rg_v(c):
-            if not ok(c) or c >= HEAD:
+            if not ok(c):
                 return
-            hgb[c] = one.tile([P, 1024], BF16, name="hgb", tag="hgb", align_bytes=64)
-            d, s = regroup_views(hga[c], hb[c])
-            n = s_tokens(c) // 4
-            nc.vector.tensor_copy(out=d[:, n:64], in_=s[:, n:64])
-            d, s = regroup_views(hgb[c], hb[c])
-            nc.vector.tensor_copy(out=d, in_=s[:, 64:128])
-
-        def g_copy(dst, src):
-            nc.gpsimd.tensor_scalar(out=dst, in0=src, scalar1=1.0, scalar2=0.0, op0=ALU.mult, op1=ALU.add)
+            if N_V > 0:
+                d, s = regroup_views(hga[c], hb[c])
+                nc.vector.tensor_copy(out=d[:, N_S // 4 : N_A // 4], in_=s[:, N_S // 4 : N_A // 4])
+            if c < HEAD:
+                hgb[c] = one.tile([P, 2048 - 4 * N_A], BF16, name="hgb", tag="hgb", align_bytes=64)
+                d, s = regroup_views(hgb[c], hb[c])
+                nc.vector.tensor_copy(out=d, in_=s[:, N_A // 4 : 128])
 
         def rg_g(c):
             if not ok(c) or c < HEAD:
                 return
-            hgb[c] = one.tile([P, 1024], BF16, name="hgb", tag="hgb", align_bytes=64)
-            s = hb[c][:].rearrange("p (t n) -> p n t", t=4)
-            g_copy(hgb[c][:].rearrange("p (n t) -> p n t", t=4), s[:, 256:512, :])
-            n = s_tokens(c)
-            if n < 256:
-                g_copy(hga[c][:].rearrange("p (n t) -> p n t", t=4)[:, n:256, :], s[:, n:256, :])
+            hgb[c] = one.tile([P, 2048 - 4 * N_A], BF16, name="hgb", tag="hgb", align_bytes=64)
+            nc.gpsimd.tensor_scalar(
+                out=hgb[c][:].rearrange("p (n t) -> p n t", t=4),
+                in0=hb[c][:].rearrange("p (t n) -> p n t", t=4)[:, N_A:512, :],
+                scalar1=1.0,
+                scalar2=0.0,
+                op0=ALU.mult,
+                op1=ALU.add,
+            )
 
-        def qh(c, half):
+        def widths(n):
+            w = []
+            for k in (512, 256, 128, 64, 32):
+                while n >= k:
+                    w.append(k)
+                    n -= k
+            return w
+
+        def qh(c, part):
             if not ok(c):
                 return
-            if half == 0:
+            if c not in hc:
                 hc[c] = work.tile([P, 512], U32, name="hc", tag="hc", align_bytes=64)
                 hs[c] = work.tile([P, 512], U8, name="hs", tag="hs", align_bytes=64)
-            src = hga[c] if half == 0 else hgb[c]
-            cols = slice(256 * half, 256 * half + 256)
-            nc.vector.quantize_mx(out=hc[c][:, cols].bitcast(FP8X4), scales=hs[c][:, cols], in_=src[:])
+            src, w0 = (hga[c], 0) if part == "a" else (hgb[c], N_A)
+            at = 0
+            for w in widths(N_A if part == "a" else 512 - N_A):
+                nc.vector.quantize_mx(
+                    out=hc[c][:, w0 + at : w0 + at + w].bitcast(FP8X4),
+                    scales=hs[c][:, w0 + at : w0 + at + w],
+                    in_=src[:, 4 * at : 4 * (at + w)],
+                )
+                at += w
 
         def m2(c, r):
             if not ok(c):
@@ -325,11 +337,11 @@ def tile_fusedthorexpert_t_kernel(tc, x, w1, b1, w2, b2, out):
             rg_v(i + 1)
             if i == -3:
                 w_quant(1, 0)
-            qx(i + 3)
             if i == -5:
                 w_regroup(1, 0, "v", 0, 128)
-            qh(i + 1, 0)
-            qh(i + 1, 1)
+            qh(i + 1, "b")
+            qh(i + 1, "a")
+            qx(i + 3)
             if i == -3:
                 w_regroup(2, 0, "v", 0, 128)
             if i == -2:

@@ -23,11 +23,14 @@ FLOPS = 2 * E * C * H * I * 2
 
 MANUAL = True
 HEAD = 2
-W_V = 80
+W_V = 96
 W_V1 = 128
 N_S = 96
-N_V = 32
-N_A = N_S + N_V
+N_LAST = 256
+
+
+def s_tokens(c):
+    return N_LAST if c >= NCH - 1 else N_S
 
 
 def tile_fusedthorexpert_t_kernel(tc, x, w1, b1, w2, b2, out):
@@ -167,8 +170,7 @@ def tile_fusedthorexpert_t_kernel(tc, x, w1, b1, w2, b2, out):
         xs = {}
         hp = {}
         hb = {}
-        hga = {}
-        hgb = {}
+        hg = {}
         hc = {}
         hs = {}
         op = {}
@@ -236,59 +238,39 @@ def tile_fusedthorexpert_t_kernel(tc, x, w1, b1, w2, b2, out):
             )
 
         def rg_s(c):
-            if not ok(c):
+            if not ok(c) or c < HEAD:
                 return
-            hga[c] = work.tile([P, 4 * N_A], BF16, name="hga", tag="hga", align_bytes=64)
-            d, s = regroup_views(hga[c], hb[c])
-            nc.scalar.copy(out=d[:, 0 : N_S // 4], in_=s[:, 0 : N_S // 4])
+            hg[c] = one.tile([P, 2048], BF16, name="hg", tag="hg", align_bytes=64)
+            d, s = regroup_views(hg[c], hb[c])
+            n = s_tokens(c) // 4
+            nc.scalar.copy(out=d[:, 0:n], in_=s[:, 0:n])
 
         def rg_v(c):
-            if not ok(c):
+            if not ok(c) or c >= HEAD:
                 return
-            if N_V > 0:
-                d, s = regroup_views(hga[c], hb[c])
-                nc.vector.tensor_copy(out=d[:, N_S // 4 : N_A // 4], in_=s[:, N_S // 4 : N_A // 4])
-            if c < HEAD:
-                hgb[c] = one.tile([P, 2048 - 4 * N_A], BF16, name="hgb", tag="hgb", align_bytes=64)
-                d, s = regroup_views(hgb[c], hb[c])
-                nc.vector.tensor_copy(out=d, in_=s[:, N_A // 4 : 128])
+            hg[c] = one.tile([P, 2048], BF16, name="hg", tag="hg", align_bytes=64)
+            d, s = regroup_views(hg[c], hb[c])
+            nc.vector.tensor_copy(out=d, in_=s)
 
         def rg_g(c):
             if not ok(c) or c < HEAD:
                 return
-            hgb[c] = one.tile([P, 2048 - 4 * N_A], BF16, name="hgb", tag="hgb", align_bytes=64)
+            n = s_tokens(c)
             nc.gpsimd.tensor_scalar(
-                out=hgb[c][:].rearrange("p (n t) -> p n t", t=4),
-                in0=hb[c][:].rearrange("p (t n) -> p n t", t=4)[:, N_A:512, :],
+                out=hg[c][:].rearrange("p (n t) -> p n t", t=4)[:, n:512, :],
+                in0=hb[c][:].rearrange("p (t n) -> p n t", t=4)[:, n:512, :],
                 scalar1=1.0,
                 scalar2=0.0,
                 op0=ALU.mult,
                 op1=ALU.add,
             )
 
-        def widths(n):
-            w = []
-            for k in (512, 256, 128, 64, 32):
-                while n >= k:
-                    w.append(k)
-                    n -= k
-            return w
-
-        def qh(c, part):
+        def qh(c):
             if not ok(c):
                 return
-            if c not in hc:
-                hc[c] = work.tile([P, 512], U32, name="hc", tag="hc", align_bytes=64)
-                hs[c] = work.tile([P, 512], U8, name="hs", tag="hs", align_bytes=64)
-            src, w0 = (hga[c], 0) if part == "a" else (hgb[c], N_A)
-            at = 0
-            for w in widths(N_A if part == "a" else 512 - N_A):
-                nc.vector.quantize_mx(
-                    out=hc[c][:, w0 + at : w0 + at + w].bitcast(FP8X4),
-                    scales=hs[c][:, w0 + at : w0 + at + w],
-                    in_=src[:, 4 * at : 4 * (at + w)],
-                )
-                at += w
+            hc[c] = work.tile([P, 512], U32, name="hc", tag="hc", align_bytes=64)
+            hs[c] = work.tile([P, 512], U8, name="hs", tag="hs", align_bytes=64)
+            nc.vector.quantize_mx(out=hc[c][:].bitcast(FP8X4), scales=hs[c][:], in_=hg[c][:])
 
         def m2(c, r):
             if not ok(c):
@@ -330,7 +312,6 @@ def tile_fusedthorexpert_t_kernel(tc, x, w1, b1, w2, b2, out):
         b1_spread()
         for i in range(-5, NCH):
             xexit(i + 4)
-            rg_s(i + 2)
             w_prep(i, "s")
             if i >= -1:
                 w_prep(i, "v")
@@ -339,8 +320,7 @@ def tile_fusedthorexpert_t_kernel(tc, x, w1, b1, w2, b2, out):
                 w_quant(1, 0)
             if i == -5:
                 w_regroup(1, 0, "v", 0, 128)
-            qh(i + 1, "b")
-            qh(i + 1, "a")
+            qh(i + 1)
             qx(i + 3)
             if i == -3:
                 w_regroup(2, 0, "v", 0, 128)
@@ -348,14 +328,17 @@ def tile_fusedthorexpert_t_kernel(tc, x, w1, b1, w2, b2, out):
                 w_quant(2, 0)
             if i == -2:
                 w_prep(i, "v")
+            rg_s(i + 2)
             rg_g(i + 2)
             if i == -1:
                 for r in range(3):
                     m2(0, r)
-            for t in range(3):
+            for t in range(2):
                 m1(i + 3, t)
             outx(i, 0)
             m2(i, 3)
+            for t in range(2, 3):
+                m1(i + 3, t)
             gelu(i + 3, 0)
             m1(i + 3, 3)
             for t in range(1, 4):

from contextlib import ExitStack

import concourse.mybir as mybir
from concourse.masks import make_identity

F32 = mybir.dt.float32
BF16 = mybir.dt.bfloat16
U32 = mybir.dt.uint32
U8 = mybir.dt.uint8
FP8X4 = mybir.dt.float8_e4m3fn_x4
ACT = mybir.ActivationFunctionType
ALU = mybir.AluOpType

E = 4
C = 2048
H = 512
I = 512
P = 128
CH = 512
NCH = E * C // CH
PER_E = C // CH
FLOPS = 2 * E * C * H * I * 2

MANUAL = True
HEAD = 2
W_V = 96
W_V1 = 128
N_S = 96
N_LAST = 256


def s_tokens(c):
    return N_LAST if c >= NCH - 1 else N_S


def tile_fusedthorexpert_t_kernel(tc, x, w1, b1, w2, b2, out):
    nc = tc.nc
    with ExitStack() as ctx:
        if MANUAL:
            ctx.enter_context(tc.manual_schedule())
        const = ctx.enter_context(tc.tile_pool(name="const", bufs=1))
        xres = ctx.enter_context(tc.tile_pool(name="xres", bufs=1))
        wres = ctx.enter_context(tc.tile_pool(name="wres", bufs=1))
        wgp = ctx.enter_context(tc.tile_pool(name="wgp", bufs=2))
        work = ctx.enter_context(tc.tile_pool(name="work", bufs=2))
        hbp = ctx.enter_context(tc.tile_pool(name="hbp", bufs=3))
        one = ctx.enter_context(tc.tile_pool(name="one", bufs=1))
        obp = ctx.enter_context(tc.tile_pool(name="obp", bufs=4))
        ps_x = ctx.enter_context(tc.psum_pool(name="ps_x", bufs=2))
        ps_h = ctx.enter_context(tc.psum_pool(name="ps_h", bufs=3))
        ps_o = ctx.enter_context(tc.psum_pool(name="ps_o", bufs=3))

        identf = const.tile([P, P], F32, name="identf")
        make_identity(nc, identf[:])
        identb = const.tile([P, P], BF16, name="identb")
        warm = const.tile([P, 1], F32, name="warm")
        warm2 = const.tile([P, 1], F32, name="warm2")
        b1raw = const.tile([P, P], BF16, name="b1raw")
        b1t = const.tile([P, E * 4], F32, name="b1t")
        b2b = {}
        nc.vector.memset(warm[:], 0.0)
        nc.vector.memset(b1raw[:], 0.0)
        nc.sync.dma_start(out=b1raw[0 : E * 4, :], in_=b1.rearrange("e (t p) -> (e t) p", p=P))
        nc.scalar.activation(out=warm2[:], in_=warm[:], func=ACT.Gelu)
        nc.vector.tensor_copy(out=identb[:], in_=identf[:])

        xsb = {}
        wraw = {}

        def load_x(c):
            t = xres.tile([P, 4 * H], BF16, name="x%d" % c)
            nc.sync.dma_start(out=t[:], in_=x[c * CH : (c + 1) * CH, :].rearrange("(w r) k -> w (r k)", r=4))
            xsb[c] = t

        def load_x_half(c, b):
            if b == 0:
                xsb[c] = xres.tile([P, 4 * H], BF16, name="x%d" % c)
            src = x[c * CH : (c + 1) * CH, :].rearrange("(w r) k -> w r k", r=4)
            nc.sync.dma_start(
                out=xsb[c][:, 2 * b * H : 2 * (b + 1) * H].rearrange("p (r k) -> p r k", r=2),
                in_=src[:, 2 * b : 2 * (b + 1), :],
            )

        def load_w1(e):
            t = wres.tile([P, 4 * I], BF16, name="w1raw%d" % e)
            nc.sync.dma_start(
                out=t[:].rearrange("p (u m) -> p u m", u=2),
                in_=w1[e].rearrange("(u p f) i -> p u (f i)", u=2, f=2),
            )
            wraw[(1, e)] = t

        def load_w2(e):
            t = wres.tile([P, 4 * H], BF16, name="w2raw%d" % e)
            nc.sync.dma_start(
                out=t[:].rearrange("p (t h) -> p t h", t=4),
                in_=w2[e].rearrange("(t p) h -> p t h", t=4),
            )
            wraw[(2, e)] = t

        def load_b2(e):
            b2b[e] = const.tile([P, H], BF16, name="b2b%d" % e)
            nc.sync.dma_start(out=b2b[e][:], in_=b2[e].partition_broadcast(P))

        load_x_half(0, 0)
        load_w1(0)
        load_x_half(0, 1)
        load_x(1)
        load_w2(0)
        load_x(2)
        load_w1(1)
        load_x(3)
        load_w2(1)
        load_b2(0)
        load_x(4)
        load_w1(2)
        load_x(5)
        load_w2(2)
        load_x(6)
        load_x(7)

        def b1_spread():
            b1ps = ps_h.tile([P, P], BF16, name="b1ps", tag="hp")
            nc.tensor.transpose(b1ps[:], b1raw[:], identb[:])
            nc.vector.tensor_copy(out=b1t[:], in_=b1ps[:, 0 : E * 4])

        wg = {}
        wcode = {}
        wscale = {}

        def regroup_views(dst, src):
            d = dst[:].rearrange("p (c i j) -> p c j i", i=4, j=4)
            s = src[:].rearrange("p (j c i) -> p c j i", j=4, i=4)
            return d, s

        def w_regroup(which, e, eng, lo, hi):
            key = (which, e)
            if key not in wg:
                wg[key] = wgp.tile([P, 2048], BF16, name="wg", tag="wg", align_bytes=64)
            if lo >= hi:
                return
            d, s = regroup_views(wg[key], wraw[key])
            if eng == "v":
                nc.vector.tensor_copy(out=d[:, lo:hi], in_=s[:, lo:hi])
            else:
                nc.scalar.copy(out=d[:, lo:hi], in_=s[:, lo:hi])

        def w_quant(which, e):
            key = (which, e)
            wcode[key] = wres.tile([P, 512], U32, name="wc%d_%d" % key, align_bytes=64)
            wscale[key] = wres.tile([P, 512], U8, name="ws%d_%d" % key, align_bytes=64)
            nc.vector.quantize_mx(out=wcode[key][:].bitcast(FP8X4), scales=wscale[key][:], in_=wg[key][:])

        def w_prep(i, eng):
            g, k = (i + 6) // 4, (i + 6) % 4
            if not 1 <= g < E:
                return
            which = 1 + k // 2
            wv = W_V if g > 1 else W_V1
            if k % 2 == 0:
                if eng == "v":
                    w_regroup(which, g, "v", 0, wv)
                else:
                    w_regroup(which, g, "s", wv, 128)
            elif eng == "v":
                w_quant(which, g)

        xt = {}
        xg = {}
        xc = {}
        xs = {}
        hp = {}
        hb = {}
        hg = {}
        hc = {}
        hs = {}
        op = {}
        ob = {}

        def ok(c):
            return 0 <= c < NCH

        def tr(c):
            if not ok(c):
                return
            xf = xsb[c][:].bitcast(F32)
            for b in range(2):
                t = ps_x.tile([P, 512], F32, name="xt", tag="xt")
                for q in range(4):
                    col = b * 512 + q * 128
                    nc.tensor.transpose(t[:, q * 128 : (q + 1) * 128], xf[:, col : col + 128], identf[:])
                xt[(c, b)] = t

        def xexit(c):
            if not ok(c):
                return
            xg[c] = work.tile([P, 2048], BF16, name="xg", tag="xg", align_bytes=64)
            gf = xg[c][:].bitcast(F32)
            for b in range(2):
                nc.scalar.copy(
                    out=gf[:, 512 * b : 512 * (b + 1)].rearrange("p (r w u) -> p r w u", r=2, u=2),
                    in_=xt[(c, b)][:].rearrange("p (r u w) -> p r w u", r=2, u=2),
                )

        def qx(c):
            if not ok(c):
                return
            xc[c] = work.tile([P, 512], U32, name="xc", tag="xc", align_bytes=64)
            xs[c] = work.tile([P, 512], U8, name="xs", tag="xs", align_bytes=64)
            nc.vector.quantize_mx(out=xc[c][:].bitcast(FP8X4), scales=xs[c][:], in_=xg[c][:])

        def m1(c, t):
            if not ok(c):
                return
            e = c // PER_E
            hp[(c, t)] = ps_h.tile([P, 512], F32, name="hp", tag="hp")
            nc.tensor.matmul_mx(
                out=hp[(c, t)][:],
                lhsT=wcode[(1, e)][:, t * P : (t + 1) * P].bitcast(FP8X4),
                lhsT_scale=wscale[(1, e)][:, t * P : (t + 1) * P],
                rhs=xc[c][:].bitcast(FP8X4),
                rhs_scale=xs[c][:],
                start=True,
                stop=True,
            )

        def gelu(c, t):
            if not ok(c):
                return
            e = c // PER_E
            if t == 0:
                hb[c] = hbp.tile([P, 2048], BF16, name="hb", tag="hb")
            nc.scalar.activation(
                out=hb[c][:, t * 512 : (t + 1) * 512],
                in_=hp[(c, t)][:],
                func=ACT.Gelu,
                bias=b1t[:, 4 * e + t : 4 * e + t + 1],
                scale=1.0,
            )

        def rg_s(c):
            if not ok(c) or c < HEAD:
                return
            hg[c] = one.tile([P, 2048], BF16, name="hg", tag="hg", align_bytes=64)
            d, s = regroup_views(hg[c], hb[c])
            n = s_tokens(c) // 4
            nc.scalar.copy(out=d[:, 0:n], in_=s[:, 0:n])

        def rg_v(c):
            if not ok(c) or c >= HEAD:
                return
            hg[c] = one.tile([P, 2048], BF16, name="hg", tag="hg", align_bytes=64)
            d, s = regroup_views(hg[c], hb[c])
            nc.vector.tensor_copy(out=d, in_=s)

        def rg_g(c):
            if not ok(c) or c < HEAD:
                return
            n = s_tokens(c)
            nc.gpsimd.tensor_scalar(
                out=hg[c][:].rearrange("p (n t) -> p n t", t=4)[:, n:512, :],
                in0=hb[c][:].rearrange("p (t n) -> p n t", t=4)[:, n:512, :],
                scalar1=1.0,
                scalar2=0.0,
                op0=ALU.mult,
                op1=ALU.add,
            )

        def qh(c):
            if not ok(c):
                return
            hc[c] = work.tile([P, 512], U32, name="hc", tag="hc", align_bytes=64)
            hs[c] = work.tile([P, 512], U8, name="hs", tag="hs", align_bytes=64)
            nc.vector.quantize_mx(out=hc[c][:].bitcast(FP8X4), scales=hs[c][:], in_=hg[c][:])

        def m2(c, r):
            if not ok(c):
                return
            e = c // PER_E
            op[(c, r)] = ps_o.tile([P, 512], F32, name="op", tag="op")
            nc.tensor.matmul_mx(
                out=op[(c, r)][:],
                lhsT=hc[c][:, r * P : (r + 1) * P].bitcast(FP8X4),
                lhsT_scale=hs[c][:, r * P : (r + 1) * P],
                rhs=wcode[(2, e)][:].bitcast(FP8X4),
                rhs_scale=wscale[(2, e)][:],
                start=True,
                stop=True,
            )

        def outx(c, r):
            if not ok(c):
                return
            e = c // PER_E
            if r == 0:
                ob[c] = obp.tile([P, 4 * H], F32, name="ob", tag="ob")
            nc.vector.tensor_tensor(
                out=ob[c][:, r * H : (r + 1) * H],
                in0=op[(c, r)][:],
                in1=b2b[e][:],
                op=ALU.add,
            )

        def store(c, r0, r1):
            if not ok(c):
                return
            dst = out[c * CH : (c + 1) * CH, :].rearrange("(w r) h -> w r h", r=4)
            nc.sync.dma_start(
                out=dst[:, r0:r1, :],
                in_=ob[c][:, r0 * H : r1 * H].rearrange("p (r h) -> p r h", h=H),
            )

        b1_spread()
        for i in range(-5, NCH):
            xexit(i + 4)
            w_prep(i, "s")
            if i >= -1:
                w_prep(i, "v")
            rg_v(i + 1)
            if i == -3:
                w_quant(1, 0)
            if i == -5:
                w_regroup(1, 0, "v", 0, 128)
            qh(i + 1)
            qx(i + 3)
            if i == -3:
                w_regroup(2, 0, "v", 0, 128)
            if i == -2:
                w_quant(2, 0)
            if i == -2:
                w_prep(i, "v")
            rg_s(i + 2)
            rg_g(i + 2)
            if i == -1:
                for r in range(3):
                    m2(0, r)
            for t in range(2):
                m1(i + 3, t)
            outx(i, 0)
            m2(i, 3)
            for t in range(2, 3):
                m1(i + 3, t)
            gelu(i + 3, 0)
            m1(i + 3, 3)
            for t in range(1, 4):
                gelu(i + 3, t)
            if i == NCH - 1:
                store(i, 0, 1)
            outx(i, 1)
            if i == NCH - 1:
                store(i, 1, 2)
            else:
                store(i, 0, 2)
            outx(i, 2)
            if i == NCH - 1:
                store(i, 2, 3)
            outx(i, 3)
            if i == NCH - 1:
                store(i, 3, 4)
            else:
                store(i, 2, 4)
            tr(i + 5)
            if i >= 0 and i + 8 < NCH:
                load_x(i + 8)
            if i >= 0 and i % 4 == 0 and i // 4 + 1 < E:
                load_b2(i // 4 + 1)
            if i == 1:
                load_w1(3)
            if i == 2:
                load_w2(3)
            if i >= 0:
                for r in range(3):
                    m2(i + 1, r)
